import numpy as np
import ml_dtypes


def mxq(x, axis, fmt="e4m3"):
    dtype, down = {"e4m3": (ml_dtypes.float8_e4m3fn, 7), "e5m2": (ml_dtypes.float8_e5m2, 14)}[fmt]
    v = np.moveaxis(np.asarray(x, np.float32).astype(ml_dtypes.bfloat16).astype(np.float64), axis, -1)
    blocks = v.reshape(v.shape[:-1] + (-1, 32))
    amax = np.abs(blocks).max(-1, keepdims=True)
    byte = np.maximum(np.where(amax > 0, np.frexp(amax)[1] - 1 + 127, 0) - down, 1)
    scale = np.exp2(byte - 127.0)
    codes = (blocks / scale).astype(np.float32).astype(dtype).astype(np.float64)
    return np.moveaxis((codes * scale).reshape(v.shape), -1, axis)


WIDE = False


def mx_kscale(k):
    if not WIDE:
        return np.ones(k)
    levels = np.array([10, -10, 5, -5, 0])
    a = np.random.permutation(np.resize(levels, k // 512 * 4)).reshape(k // 512, 4)
    idx = np.arange(k)
    return np.exp2(a[idx // 512, idx % 128 // 32])


BF16 = ml_dtypes.bfloat16


def bf(x):
    return np.asarray(x, np.float32).astype(BF16)


def f64(x):
    return np.asarray(x).astype(np.float64)


E2M1 = np.array([0.0, 0.5, 1.0, 1.5, 2.0, 3.0, 4.0, 6.0, -0.0, -0.5, -1.0, -1.5, -2.0, -3.0, -4.0, -6.0])


def pack_weight(w, fmt):
    k, n = w.shape
    w = f64(bf(w)).reshape(k // 32, 32, n)
    amax = np.abs(w).max(1)
    if fmt == "e4m3":
        byte = np.frexp(amax)[1] - 1 + 127 - 7
    else:
        mant, ex = np.frexp(amax / 6.0)
        byte = np.where(mant > 0.5, ex, ex - 1) + 127
    byte = np.clip(np.where(amax > 0, byte, 1), 1, 254)
    scaled = (w * np.exp2(127.0 - byte)[:, None, :]).reshape(k, n).astype(np.float32)
    by_word = np.ascontiguousarray(scaled.reshape(k // 512, 128, 4, n).transpose(0, 1, 3, 2))
    if fmt == "e4m3":
        words = by_word.astype(ml_dtypes.float8_e4m3fn).view(np.uint8)
    else:
        c = by_word.astype(ml_dtypes.float4_e2m1fn).view(np.uint8) & 0xF
        words = c[..., 0::2] | (c[..., 1::2] << 4)
    return np.ascontiguousarray(words), np.ascontiguousarray(byte.astype(np.uint8).reshape(k // 512, 16, n))


def unpack_weight(words, scales, fmt):
    g, p, n, _ = words.shape
    if fmt == "e4m3":
        vals = np.ascontiguousarray(words).view(ml_dtypes.float8_e4m3fn).astype(np.float64)
    else:
        nib = np.empty((g, p, n, 4), np.uint8)
        nib[..., 0::2] = words & 0xF
        nib[..., 1::2] = words >> 4
        vals = E2M1[nib]
    vals = vals * np.repeat(np.exp2(scales.astype(np.float64) - 127.0), 8, axis=1)[..., None]
    return vals.transpose(0, 1, 3, 2).reshape(g * 512, n)


B, C, HH, WW, NH, HD, F = 4, 8192, 8, 8, 8, 64, 1024
E = NH * HD


def setup_inputs():
    s, t = mx_kscale(E), mx_kscale(C)
    o = bf(np.random.standard_normal((B, HH, WW, E)) * 0.6 * s)
    xn = bf(np.random.standard_normal((B, HH, WW, C)) * 0.5 * t)
    W_O_words, W_O_scales = pack_weight(np.random.standard_normal((E, C)) / np.sqrt(E) / s[:, None] * t, "e4m3")
    scale_attn = bf(0.5 * (1.0 + 0.1 * np.random.standard_normal(1)))
    ffn1_w_words, ffn1_w_scales = pack_weight((np.random.standard_normal((F, C)) * 3.0 / np.sqrt(C) / t).T, "e4m3")
    ffn1_b = bf(np.random.standard_normal(F) * 0.3)
    scale_ffn = bf(0.1 * (1.0 + 0.1 * np.random.standard_normal(1)))
    return {"o": o,
            "xn": xn,
            "W_O_words": W_O_words,
            "W_O_scales": W_O_scales,
            "scale_attn": scale_attn,
            "ffn1_w_words": ffn1_w_words,
            "ffn1_w_scales": ffn1_w_scales,
            "ffn1_b": ffn1_b,
            "scale_ffn": scale_ffn}


def reference(o, xn, W_O_words, W_O_scales, scale_attn, ffn1_w_words, ffn1_w_scales, ffn1_b, scale_ffn):
    p = (mxq(f64(o), 3, "e4m3") @ unpack_weight(W_O_words, W_O_scales, "e4m3")) * f64(scale_attn)
    y = np.maximum(f64(xn) + p, 0.0)
    u = (mxq(y, 3, "e4m3") @ unpack_weight(ffn1_w_words, ffn1_w_scales, "e4m3")) + f64(ffn1_b)
    return np.maximum(u * f64(scale_ffn), 0.0)

@@ -1,0 +1,240 @@
+import concourse.mybir as mybir
+from concourse.masks import make_identity
+
+F32 = mybir.dt.float32
+BF16 = mybir.dt.bfloat16
+I32 = mybir.dt.int32
+U32 = mybir.dt.uint32
+U8 = mybir.dt.uint8
+FP8X4 = mybir.dt.float8_e4m3fn_x4
+ALU = mybir.AluOpType
+ACT = mybir.ActivationFunctionType
+
+P = 128
+TOKENS = 256
+TOKEN_TILES = TOKENS // P
+K_PASS = 4 * P
+CHANNELS = 8192
+GROUPS = CHANNELS // K_PASS
+PAIRS = GROUPS // 2
+FFN = 1024
+BANK = 512
+FFN_HALVES = FFN // BANK
+PLANES = 4
+STAGE2_START = 3
+
+FLOPS = 2 * TOKENS * K_PASS * CHANNELS + 2 * TOKENS * CHANNELS * FFN
+
+
+def tile_transformerconvblock_pb_k_kernel(
+    tc, o, xn, W_O_words, W_O_scales, scale_attn, ffn1_w_words, ffn1_w_scales, ffn1_b, scale_ffn, out
+):
+    nc = tc.nc
+    o_rows = o.flatten_outer_dims().rearrange("(i p) k -> p i k", p=P)
+    xn_rows = xn.flatten_outer_dims().rearrange("(i p) c -> p i c", p=P)
+    out_rows = out.flatten_outer_dims()
+    wo_words_in = W_O_words.rearrange("g p n t -> (g p) (n t)").bitcast(I32)
+    wo_scales_in = W_O_scales.rearrange("g q (k x) -> (g k) q x", k=PLANES)
+    ffn_words_in = ffn1_w_words.rearrange("g p n t -> p g (n t)").bitcast(I32)
+
+    with tc.manual_schedule(), tc.tile_pool(name="resident", bufs=1) as resident, tc.tile_pool(
+        name="work", bufs=4
+    ) as work, tc.psum_pool(name="psum_stage1", bufs=2) as psum_stage1, tc.psum_pool(
+        name="psum_turned", bufs=2
+    ) as psum_turned, tc.psum_pool(name="psum_acc", bufs=1) as psum_acc:
+        wo_planes = resident.tile([P, CHANNELS // PLANES], U8, align_bytes=64)
+        ffn_planes = resident.tile([P, GROUPS // PLANES, FFN], U8, align_bytes=64)
+        nc.vector.memset(wo_planes[:].bitcast(I32), 0)
+        nc.vector.memset(ffn_planes[:].rearrange("p b n -> p (b n)").bitcast(I32), 0)
+        bias_row = resident.tile([P, FFN], BF16)
+        nc.vector.memset(bias_row[:], 0.0)
+        ones = resident.tile([P, P], BF16)
+        nc.vector.memset(ones[:], 1.0)
+        identity = resident.tile([P, P], F32)
+        make_identity(nc, identity[:])
+
+        attn_bf16 = resident.tile([P, 1], BF16)
+        ffn_bf16 = resident.tile([P, 1], BF16)
+        nc.scalar.dma_start(out=attn_bf16[:], in_=scale_attn.partition_broadcast(P))
+        nc.scalar.dma_start(out=ffn_bf16[:], in_=scale_ffn.partition_broadcast(P))
+        nc.scalar.dma_start(out=bias_row[0:1, :], in_=ffn1_b.unsqueeze(0))
+
+        o_sb = resident.tile([P, TOKEN_TILES, K_PASS], BF16)
+        nc.sync.dma_start(out=o_sb[:], in_=o_rows)
+        for quadrant in range(4):
+            nc.sync.dma_start(
+                out=wo_planes[32 * quadrant : 32 * quadrant + 16, :].bitcast(I32),
+                in_=wo_scales_in[:, 4 * quadrant : 4 * quadrant + 4, :].bitcast(I32),
+            )
+
+        xn_sb = []
+        wo_words = []
+        ffn_words = []
+
+        def load_pair(pair):
+            channels = slice(2 * K_PASS * pair, 2 * K_PASS * (pair + 1))
+            xn_pair = resident.tile([P, TOKEN_TILES, 2 * K_PASS], BF16, name="xn%d" % pair)
+            nc.sync.dma_start(out=xn_pair[:], in_=xn_rows[:, :, channels])
+            xn_sb.append(xn_pair)
+            wo_pair = resident.tile([P, 4 * 2 * K_PASS], U8, name="wo%d" % pair, align_bytes=64)
+            nc.sync.dma_start(out=wo_pair[:].bitcast(I32), in_=wo_words_in[:, channels])
+            wo_words.append(wo_pair)
+
+        def load_ffn_group(group):
+            ffn_group = resident.tile([P, 4 * FFN], U8, name="ffn%d" % group, align_bytes=64)
+            nc.sync.dma_start(out=ffn_group[:].bitcast(I32), in_=ffn_words_in[:, group, :])
+            ffn_words.append(ffn_group)
+
+        for pair in range(STAGE2_START):
+            load_pair(pair)
+        for block in range(GROUPS // PLANES):
+            for quadrant in range(4):
+                nc.sync.dma_start(
+                    out=ffn_planes[32 * quadrant : 32 * quadrant + 16, block, :].bitcast(I32),
+                    in_=ffn1_w_scales[
+                        PLANES * block : PLANES * (block + 1), 4 * quadrant : 4 * quadrant + 4, :
+                    ].bitcast(I32),
+                )
+        for pair in range(STAGE2_START, PAIRS):
+            load_pair(pair)
+            load_ffn_group(pair - STAGE2_START)
+        for group in range(PAIRS - STAGE2_START, GROUPS):
+            load_ffn_group(group)
+
+        attn_scale = resident.tile([P, 1], F32)
+        ffn_scale = resident.tile([P, 1], F32)
+        nc.vector.tensor_copy(out=attn_scale[:], in_=attn_bf16[:])
+        nc.vector.tensor_copy(out=ffn_scale[:], in_=ffn_bf16[:])
+
+        o_turned = psum_turned.tile([P, 2, TOKENS], F32, tag="turned")
+        for i in range(TOKEN_TILES):
+            o_as_words = o_sb[:, i, :].bitcast(F32)
+            for u in range(2):
+                nc.tensor.transpose(
+                    o_turned[:, u, P * i : P * (i + 1)], o_as_words[:, u : K_PASS // 2 : 2], identity[:]
+                )
+        o_grouped = work.tile([P, TOKENS, 2, 2], BF16, tag="grouped", align_bytes=64)
+        nc.vector.tensor_copy(
+            out=o_grouped[:].rearrange("p k u e -> p k (u e)").bitcast(F32),
+            in_=o_turned[:].rearrange("p u k -> p k u"),
+        )
+        o_codes = resident.tile([P, TOKENS], U32, align_bytes=64)
+        o_plane = resident.tile([P, TOKENS], U8, align_bytes=64)
+        nc.vector.quantize_mx(
+            out=o_codes[:].bitcast(FP8X4),
+            scales=o_plane[:],
+            in_=o_grouped[:].rearrange("p k u e -> p (k u e)"),
+        )
+
+        bias_all = resident.tile([P, FFN], F32)
+        for h in range(FFN_HALVES):
+            spread = psum_stage1.tile([P, BANK], F32, tag="stage1")
+            nc.tensor.matmul(
+                out=spread[:], lhsT=ones[:], rhs=bias_row[:, BANK * h : BANK * (h + 1)], start=True, stop=True
+            )
+            nc.scalar.copy(out=bias_all[:, BANK * h : BANK * (h + 1)], in_=spread[:])
+
+        summed = {}
+        grouped = {}
+        y_codes = {}
+        y_planes = {}
+        acc = [
+            [psum_acc.tile([P, BANK], F32, name="acc%d%d" % (i, h)) for h in range(FFN_HALVES)]
+            for i in range(TOKEN_TILES)
+        ]
+
+        def stage1(group):
+            pair, half = divmod(group, 2)
+            plane, quarter = divmod(group, PLANES)
+            z = work.tile([P, TOKEN_TILES, 2, 2 * P], BF16, tag="summed")
+            for i in range(TOKEN_TILES):
+                product = psum_stage1.tile([P, BANK], F32, tag="stage1")
+                nc.tensor.matmul_mx(
+                    out=product[:],
+                    lhsT=o_codes[:, P * i : P * (i + 1)].bitcast(FP8X4),
+                    lhsT_scale=o_plane[:, P * i : P * (i + 1)],
+                    rhs=wo_words[pair][:, 4 * K_PASS * half : 4 * K_PASS * (half + 1)].bitcast(FP8X4),
+                    rhs_scale=wo_planes[4 * plane : P, K_PASS * quarter : K_PASS * (quarter + 1)],
+                    start=True,
+                    stop=True,
+                )
+                residual = xn_sb[pair][:, i, K_PASS * half : K_PASS * (half + 1)]
+                for u in range(2):
+                    nc.vector.scalar_tensor_tensor(
+                        out=z[:, i, u, :].rearrange("k (p e) -> k p e", e=2),
+                        in0=product[:].rearrange("k (p u e) -> k u p e", u=2, e=2)[:, u],
+                        scalar=attn_scale[:, 0:1],
+                        in1=residual.rearrange("k (p u e) -> k u p e", u=2, e=2)[:, u],
+                        op0=ALU.mult,
+                        op1=ALU.add,
+                    )
+            summed[group] = z
+
+        def turn(group):
+            z = summed[group]
+            turned = psum_turned.tile([P, 2, TOKENS], F32, tag="turned")
+            for i in range(TOKEN_TILES):
+                for u in range(2):
+                    nc.tensor.transpose(turned[:, u, P * i : P * (i + 1)], z[:, i, u, :].bitcast(F32), identity[:])
+            y = work.tile([P, TOKENS, 2, 2], BF16, tag="grouped", align_bytes=64)
+            nc.scalar.activation(
+                out=y[:],
+                in_=turned[:].bitcast(BF16).rearrange("p u (k e) -> p k u e", e=2),
+                func=ACT.Relu,
+            )
+            grouped[group] = y
+
+        def quantise(group):
+            codes = resident.tile([P, TOKENS], U32, name="y_codes%d" % group, align_bytes=64)
+            plane = resident.tile([P, TOKENS], U8, name="y_plane%d" % group, align_bytes=64)
+            nc.vector.quantize_mx(
+                out=codes[:].bitcast(FP8X4),
+                scales=plane[:],
+                in_=grouped[group][:].rearrange("p k u e -> p (k u e)"),
+            )
+            y_codes[group] = codes
+            y_planes[group] = plane
+
+        def stage2(group):
+            block, plane = divmod(group, PLANES)
+            for i in range(TOKEN_TILES):
+                for h in range(FFN_HALVES):
+                    nc.tensor.matmul_mx(
+                        out=acc[i][h][:],
+                        lhsT=y_codes[group][:, P * i : P * (i + 1)].bitcast(FP8X4),
+                        lhsT_scale=y_planes[group][:, P * i : P * (i + 1)],
+                        rhs=ffn_words[group][:, 4 * BANK * h : 4 * BANK * (h + 1)].bitcast(FP8X4),
+                        rhs_scale=ffn_planes[4 * plane : P, block, BANK * h : BANK * (h + 1)],
+                        start=(group == 0),
+                        stop=(group == GROUPS - 1),
+                    )
+
+        for step in range(PAIRS + 1):
+            if step < PAIRS:
+                stage1(2 * step)
+            if step >= 2:
+                quantise(2 * (step - 2))
+            if step >= STAGE2_START:
+                stage2(step - STAGE2_START)
+            if step < PAIRS:
+                stage1(2 * step + 1)
+            if step >= 2:
+                quantise(2 * (step - 2) + 1)
+            if step >= 1:
+                turn(2 * (step - 1))
+                turn(2 * (step - 1) + 1)
+        quantise(GROUPS - 2)
+        quantise(GROUPS - 1)
+
+        for group in range(PAIRS + 1 - STAGE2_START, GROUPS):
+            stage2(group)
+
+        for i in range(TOKEN_TILES):
+            for h in range(FFN_HALVES):
+                biased = work.tile([P, BANK], F32, tag="biased")
+                nc.vector.tensor_tensor(
+                    out=biased[:], in0=acc[i][h][:], in1=bias_all[:, BANK * h : BANK * (h + 1)], op=ALU.add
+                )
+                result = work.tile([P, BANK], F32, tag="result")
+                nc.scalar.activation(out=result[:], in_=biased[:], func=ACT.Relu, scale=ffn_scale[:, 0:1])
+                nc.sync.dma_start(out=out_rows[P * i : P * (i + 1), BANK * h : BANK * (h + 1)], in_=result[:])

@@ -21,7 +21,8 @@ FFN = 1024
 BANK = 512
 FFN_HALVES = FFN // BANK
 PLANES = 4
-STAGE2_START = 3
+TURN_LAG = 0
+STEPS = PAIRS + 2 + TURN_LAG
 
 FLOPS = 2 * TOKENS * K_PASS * CHANNELS + 2 * TOKENS * CHANNELS * FFN
 
@@ -53,14 +54,13 @@ def tile_transformerconvblock_pb_k_kernel(
         identity = resident.tile([P, P], F32)
         make_identity(nc, identity[:])
 
-        attn_bf16 = resident.tile([P, 1], BF16)
-        ffn_bf16 = resident.tile([P, 1], BF16)
-        nc.scalar.dma_start(out=attn_bf16[:], in_=scale_attn.partition_broadcast(P))
-        nc.scalar.dma_start(out=ffn_bf16[:], in_=scale_ffn.partition_broadcast(P))
-        nc.scalar.dma_start(out=bias_row[0:1, :], in_=ffn1_b.unsqueeze(0))
+        def quantised_in(step):
+            return 2 * (step - 1 - TURN_LAG)
 
         o_sb = resident.tile([P, TOKEN_TILES, K_PASS], BF16)
         nc.sync.dma_start(out=o_sb[:], in_=o_rows)
+        attn_bf16 = resident.tile([P, 1], BF16)
+        nc.sync.dma_start(out=attn_bf16[:], in_=scale_attn.partition_broadcast(P))
         for quadrant in range(4):
             nc.sync.dma_start(
                 out=wo_planes[32 * quadrant : 32 * quadrant + 16, :].bitcast(I32),
@@ -70,41 +70,36 @@ def tile_transformerconvblock_pb_k_kernel(
         xn_sb = []
         wo_words = []
         ffn_words = []
-
-        def load_pair(pair):
-            channels = slice(2 * K_PASS * pair, 2 * K_PASS * (pair + 1))
-            xn_pair = resident.tile([P, TOKEN_TILES, 2 * K_PASS], BF16, name="xn%d" % pair)
-            nc.sync.dma_start(out=xn_pair[:], in_=xn_rows[:, :, channels])
-            xn_sb.append(xn_pair)
-            wo_pair = resident.tile([P, 4 * 2 * K_PASS], U8, name="wo%d" % pair, align_bytes=64)
-            nc.sync.dma_start(out=wo_pair[:].bitcast(I32), in_=wo_words_in[:, channels])
-            wo_words.append(wo_pair)
-
-        def load_ffn_group(group):
-            ffn_group = resident.tile([P, 4 * FFN], U8, name="ffn%d" % group, align_bytes=64)
-            nc.sync.dma_start(out=ffn_group[:].bitcast(I32), in_=ffn_words_in[:, group, :])
-            ffn_words.append(ffn_group)
-
-        for pair in range(STAGE2_START):
-            load_pair(pair)
-        for block in range(GROUPS // PLANES):
-            for quadrant in range(4):
-                nc.sync.dma_start(
-                    out=ffn_planes[32 * quadrant : 32 * quadrant + 16, block, :].bitcast(I32),
-                    in_=ffn1_w_scales[
-                        PLANES * block : PLANES * (block + 1), 4 * quadrant : 4 * quadrant + 4, :
-                    ].bitcast(I32),
-                )
-        for pair in range(STAGE2_START, PAIRS):
-            load_pair(pair)
-            load_ffn_group(pair - STAGE2_START)
-        for group in range(PAIRS - STAGE2_START, GROUPS):
-            load_ffn_group(group)
+        ffn_bf16 = resident.tile([P, 1], BF16)
+        for step in range(STEPS):
+            if step < PAIRS:
+                channels = slice(2 * K_PASS * step, 2 * K_PASS * (step + 1))
+                wo_pair = resident.tile([P, 4 * 2 * K_PASS], U8, name="wo%d" % step, align_bytes=64)
+                nc.sync.dma_start(out=wo_pair[:].bitcast(I32), in_=wo_words_in[:, channels])
+                wo_words.append(wo_pair)
+                xn_pair = resident.tile([P, TOKEN_TILES, 2 * K_PASS], BF16, name="xn%d" % step)
+                nc.sync.dma_start(out=xn_pair[:], in_=xn_rows[:, :, channels])
+                xn_sb.append(xn_pair)
+            if step == 0:
+                nc.sync.dma_start(out=bias_row[0:1, :], in_=ffn1_b.unsqueeze(0))
+                nc.sync.dma_start(out=ffn_bf16[:], in_=scale_ffn.partition_broadcast(P))
+            if quantised_in(step) == 0:
+                for block in range(GROUPS // PLANES):
+                    for quadrant in range(4):
+                        nc.sync.dma_start(
+                            out=ffn_planes[32 * quadrant : 32 * quadrant + 16, block, :].bitcast(I32),
+                            in_=ffn1_w_scales[
+                                PLANES * block : PLANES * (block + 1), 4 * quadrant : 4 * quadrant + 4, :
+                            ].bitcast(I32),
+                        )
+            for group in (quantised_in(step) - 1, quantised_in(step)):
+                if 0 <= group < GROUPS:
+                    ffn_group = resident.tile([P, 4 * FFN], U8, name="ffn%d" % group, align_bytes=64)
+                    nc.sync.dma_start(out=ffn_group[:].bitcast(I32), in_=ffn_words_in[:, group, :])
+                    ffn_words.append(ffn_group)
 
         attn_scale = resident.tile([P, 1], F32)
-        ffn_scale = resident.tile([P, 1], F32)
         nc.vector.tensor_copy(out=attn_scale[:], in_=attn_bf16[:])
-        nc.vector.tensor_copy(out=ffn_scale[:], in_=ffn_bf16[:])
 
         o_turned = psum_turned.tile([P, 2, TOKENS], F32, tag="turned")
         for i in range(TOKEN_TILES):
@@ -126,14 +121,6 @@ def tile_transformerconvblock_pb_k_kernel(
             in_=o_grouped[:].rearrange("p k u e -> p (k u e)"),
         )
 
-        bias_all = resident.tile([P, FFN], F32)
-        for h in range(FFN_HALVES):
-            spread = psum_stage1.tile([P, BANK], F32, tag="stage1")
-            nc.tensor.matmul(
-                out=spread[:], lhsT=ones[:], rhs=bias_row[:, BANK * h : BANK * (h + 1)], start=True, stop=True
-            )
-            nc.scalar.copy(out=bias_all[:, BANK * h : BANK * (h + 1)], in_=spread[:])
-
         summed = {}
         grouped = {}
         y_codes = {}
@@ -142,6 +129,17 @@ def tile_transformerconvblock_pb_k_kernel(
             [psum_acc.tile([P, BANK], F32, name="acc%d%d" % (i, h)) for h in range(FFN_HALVES)]
             for i in range(TOKEN_TILES)
         ]
+
+        bias_all = resident.tile([P, FFN], F32)
+        ffn_scale = resident.tile([P, 1], F32)
+
+        def prepare_last_lines():
+            nc.vector.tensor_copy(out=ffn_scale[:], in_=ffn_bf16[:])
+            for h in range(FFN_HALVES):
+                nc.tensor.matmul(
+                    out=acc[0][h][:], lhsT=ones[:], rhs=bias_row[:, BANK * h : BANK * (h + 1)], start=True, stop=True
+                )
+                nc.scalar.copy(out=bias_all[:, BANK * h : BANK * (h + 1)], in_=acc[0][h][:])
 
         def stage1(group):
             pair, half = divmod(group, 2)
@@ -209,25 +207,19 @@ def tile_transformerconvblock_pb_k_kernel(
                         stop=(group == GROUPS - 1),
                     )
 
-        for step in range(PAIRS + 1):
-            if step < PAIRS:
-                stage1(2 * step)
-            if step >= 2:
-                quantise(2 * (step - 2))
-            if step >= STAGE2_START:
-                stage2(step - STAGE2_START)
-            if step < PAIRS:
-                stage1(2 * step + 1)
-            if step >= 2:
-                quantise(2 * (step - 2) + 1)
-            if step >= 1:
-                turn(2 * (step - 1))
-                turn(2 * (step - 1) + 1)
-        quantise(GROUPS - 2)
-        quantise(GROUPS - 1)
-
-        for group in range(PAIRS + 1 - STAGE2_START, GROUPS):
-            stage2(group)
+        for step in range(STEPS):
+            for half in range(2):
+                if step < PAIRS:
+                    stage1(2 * step + half)
+                if 0 <= quantised_in(step) + half < GROUPS:
+                    quantise(quantised_in(step) + half)
+                if 0 <= quantised_in(step) + half - 1 < GROUPS:
+                    stage2(quantised_in(step) + half - 1)
+            if step == 0:
+                prepare_last_lines()
+            if 0 <= step - TURN_LAG < PAIRS:
+                turn(2 * (step - TURN_LAG))
+                turn(2 * (step - TURN_LAG) + 1)
 
         for i in range(TOKEN_TILES):
             for h in range(FFN_HALVES):

@@ -44,9 +44,12 @@ def tile_transformerconvblock_pb_k_kernel(
         name="psum_turned", bufs=2
     ) as psum_turned, tc.psum_pool(name="psum_acc", bufs=1) as psum_acc:
         wo_planes = resident.tile([P, CHANNELS // PLANES], U8, align_bytes=64)
-        ffn_planes = resident.tile([P, GROUPS // PLANES, FFN], U8, align_bytes=64)
         nc.vector.memset(wo_planes[:].bitcast(I32), 0)
-        nc.vector.memset(ffn_planes[:].rearrange("p b n -> p (b n)").bitcast(I32), 0)
+        ffn_planes = []
+        for block in range(GROUPS // PLANES):
+            block_planes = resident.tile([P, FFN], U8, name="ffn_planes%d" % block, align_bytes=64)
+            nc.vector.memset(block_planes[:].bitcast(I32), 0)
+            ffn_planes.append(block_planes)
         bias_row = resident.tile([P, FFN], BF16)
         nc.vector.memset(bias_row[:], 0.0)
         ones = resident.tile([P, P], BF16)
@@ -54,13 +57,17 @@ def tile_transformerconvblock_pb_k_kernel(
         identity = resident.tile([P, P], F32)
         make_identity(nc, identity[:])
 
+        attn_bf16 = resident.tile([P, 1], BF16)
+        ffn_bf16 = resident.tile([P, 1], BF16)
+        nc.gpsimd.dma_start(out=attn_bf16[:], in_=scale_attn.partition_broadcast(P))
+        nc.gpsimd.dma_start(out=bias_row[0:1, :], in_=ffn1_b.unsqueeze(0))
+        nc.gpsimd.dma_start(out=ffn_bf16[:], in_=scale_ffn.partition_broadcast(P))
+
         def quantised_in(step):
             return 2 * (step - 1 - TURN_LAG)
 
         o_sb = resident.tile([P, TOKEN_TILES, K_PASS], BF16)
         nc.sync.dma_start(out=o_sb[:], in_=o_rows)
-        attn_bf16 = resident.tile([P, 1], BF16)
-        nc.sync.dma_start(out=attn_bf16[:], in_=scale_attn.partition_broadcast(P))
         for quadrant in range(4):
             nc.sync.dma_start(
                 out=wo_planes[32 * quadrant : 32 * quadrant + 16, :].bitcast(I32),
@@ -70,7 +77,6 @@ def tile_transformerconvblock_pb_k_kernel(
         xn_sb = []
         wo_words = []
         ffn_words = []
-        ffn_bf16 = resident.tile([P, 1], BF16)
         for step in range(STEPS):
             if step < PAIRS:
                 channels = slice(2 * K_PASS * step, 2 * K_PASS * (step + 1))
@@ -80,20 +86,16 @@ def tile_transformerconvblock_pb_k_kernel(
                 xn_pair = resident.tile([P, TOKEN_TILES, 2 * K_PASS], BF16, name="xn%d" % step)
                 nc.sync.dma_start(out=xn_pair[:], in_=xn_rows[:, :, channels])
                 xn_sb.append(xn_pair)
-            if step == 0:
-                nc.sync.dma_start(out=bias_row[0:1, :], in_=ffn1_b.unsqueeze(0))
-                nc.sync.dma_start(out=ffn_bf16[:], in_=scale_ffn.partition_broadcast(P))
-            if quantised_in(step) == 0:
-                for block in range(GROUPS // PLANES):
-                    for quadrant in range(4):
-                        nc.sync.dma_start(
-                            out=ffn_planes[32 * quadrant : 32 * quadrant + 16, block, :].bitcast(I32),
-                            in_=ffn1_w_scales[
-                                PLANES * block : PLANES * (block + 1), 4 * quadrant : 4 * quadrant + 4, :
-                            ].bitcast(I32),
-                        )
             for group in (quantised_in(step) - 1, quantised_in(step)):
                 if 0 <= group < GROUPS:
+                    if group % PLANES == 0:
+                        for quadrant in range(4):
+                            nc.sync.dma_start(
+                                out=ffn_planes[group // PLANES][32 * quadrant : 32 * quadrant + 16, :].bitcast(I32),
+                                in_=ffn1_w_scales[
+                                    group : group + PLANES, 4 * quadrant : 4 * quadrant + 4, :
+                                ].bitcast(I32),
+                            )
                     ffn_group = resident.tile([P, 4 * FFN], U8, name="ffn%d" % group, align_bytes=64)
                     nc.sync.dma_start(out=ffn_group[:].bitcast(I32), in_=ffn_words_in[:, group, :])
                     ffn_words.append(ffn_group)
@@ -202,7 +204,7 @@ def tile_transformerconvblock_pb_k_kernel(
                         lhsT=y_codes[group][:, P * i : P * (i + 1)].bitcast(FP8X4),
                         lhsT_scale=y_planes[group][:, P * i : P * (i + 1)],
                         rhs=ffn_words[group][:, 4 * BANK * h : 4 * BANK * (h + 1)].bitcast(FP8X4),
-                        rhs_scale=ffn_planes[4 * plane : P, block, BANK * h : BANK * (h + 1)],
+                        rhs_scale=ffn_planes[block][4 * plane : P, BANK * h : BANK * (h + 1)],
                         start=(group == 0),
                         stop=(group == GROUPS - 1),
                     )

@@ -21,8 +21,9 @@ FFN = 1024
 BANK = 512
 FFN_HALVES = FFN // BANK
 PLANES = 4
-TURN_LAG = 0
-STEPS = PAIRS + 2 + TURN_LAG
+STAGE2_LAG = 5
+TAPERED = 2
+STEPS = (GROUPS - TAPERED + STAGE2_LAG + 1) // 2
 
 FLOPS = 2 * TOKENS * K_PASS * CHANNELS + 2 * TOKENS * CHANNELS * FFN
 
@@ -59,12 +60,9 @@ def tile_transformerconvblock_pb_k_kernel(
 
         attn_bf16 = resident.tile([P, 1], BF16)
         ffn_bf16 = resident.tile([P, 1], BF16)
-        nc.gpsimd.dma_start(out=attn_bf16[:], in_=scale_attn.partition_broadcast(P))
+        nc.scalar.dma_start(out=attn_bf16[:], in_=scale_attn.partition_broadcast(P))
         nc.gpsimd.dma_start(out=bias_row[0:1, :], in_=ffn1_b.unsqueeze(0))
         nc.gpsimd.dma_start(out=ffn_bf16[:], in_=scale_ffn.partition_broadcast(P))
-
-        def quantised_in(step):
-            return 2 * (step - 1 - TURN_LAG)
 
         o_sb = resident.tile([P, TOKEN_TILES, K_PASS], BF16)
         nc.sync.dma_start(out=o_sb[:], in_=o_rows)
@@ -76,7 +74,8 @@ def tile_transformerconvblock_pb_k_kernel(
 
         xn_sb = []
         wo_words = []
-        ffn_words = []
+        ffn_words = {}
+
         for step in range(STEPS):
             if step < PAIRS:
                 channels = slice(2 * K_PASS * step, 2 * K_PASS * (step + 1))
@@ -86,8 +85,8 @@ def tile_transformerconvblock_pb_k_kernel(
                 xn_pair = resident.tile([P, TOKEN_TILES, 2 * K_PASS], BF16, name="xn%d" % step)
                 nc.sync.dma_start(out=xn_pair[:], in_=xn_rows[:, :, channels])
                 xn_sb.append(xn_pair)
-            for group in (quantised_in(step) - 1, quantised_in(step)):
-                if 0 <= group < GROUPS:
+            for group in (2 * step - STAGE2_LAG, 2 * step - STAGE2_LAG + 1):
+                if 0 <= group < GROUPS - TAPERED:
                     if group % PLANES == 0:
                         for quadrant in range(4):
                             nc.sync.dma_start(
@@ -96,9 +95,15 @@ def tile_transformerconvblock_pb_k_kernel(
                                     group : group + PLANES, 4 * quadrant : 4 * quadrant + 4, :
                                 ].bitcast(I32),
                             )
-                    ffn_group = resident.tile([P, 4 * FFN], U8, name="ffn%d" % group, align_bytes=64)
-                    nc.sync.dma_start(out=ffn_group[:].bitcast(I32), in_=ffn_words_in[:, group, :])
-                    ffn_words.append(ffn_group)
+                    whole = resident.tile([P, 4 * FFN], U8, name="ffn%d" % group, align_bytes=64)
+                    nc.sync.dma_start(out=whole[:].bitcast(I32), in_=ffn_words_in[:, group, :])
+                    for h in range(FFN_HALVES):
+                        ffn_words[(group, h)] = whole[:, 4 * BANK * h : 4 * BANK * (h + 1)]
+        for h in range(FFN_HALVES):
+            for group in range(GROUPS - TAPERED, GROUPS):
+                part = resident.tile([P, 4 * BANK], U8, name="ffn%d_%d" % (group, h), align_bytes=64)
+                nc.sync.dma_start(out=part[:].bitcast(I32), in_=ffn_words_in[:, group, BANK * h : BANK * (h + 1)])
+                ffn_words[(group, h)] = part[:]
 
         attn_scale = resident.tile([P, 1], F32)
         nc.vector.tensor_copy(out=attn_scale[:], in_=attn_bf16[:])
@@ -195,36 +200,21 @@ def tile_transformerconvblock_pb_k_kernel(
             y_codes[group] = codes
             y_planes[group] = plane
 
-        def stage2(group):
+        def stage2(group, h):
             block, plane = divmod(group, PLANES)
             for i in range(TOKEN_TILES):
-                for h in range(FFN_HALVES):
-                    nc.tensor.matmul_mx(
-                        out=acc[i][h][:],
-                        lhsT=y_codes[group][:, P * i : P * (i + 1)].bitcast(FP8X4),
-                        lhsT_scale=y_planes[group][:, P * i : P * (i + 1)],
-                        rhs=ffn_words[group][:, 4 * BANK * h : 4 * BANK * (h + 1)].bitcast(FP8X4),
-                        rhs_scale=ffn_planes[block][4 * plane : P, BANK * h : BANK * (h + 1)],
-                        start=(group == 0),
-                        stop=(group == GROUPS - 1),
-                    )
+                nc.tensor.matmul_mx(
+                    out=acc[i][h][:],
+                    lhsT=y_codes[group][:, P * i : P * (i + 1)].bitcast(FP8X4),
+                    lhsT_scale=y_planes[group][:, P * i : P * (i + 1)],
+                    rhs=ffn_words[(group, h)].bitcast(FP8X4),
+                    rhs_scale=ffn_planes[block][4 * plane : P, BANK * h : BANK * (h + 1)],
+                    start=(group == 0),
+                    stop=(group == GROUPS - 1),
+                )
 
-        for step in range(STEPS):
-            for half in range(2):
-                if step < PAIRS:
-                    stage1(2 * step + half)
-                if 0 <= quantised_in(step) + half < GROUPS:
-                    quantise(quantised_in(step) + half)
-                if 0 <= quantised_in(step) + half - 1 < GROUPS:
-                    stage2(quantised_in(step) + half - 1)
-            if step == 0:
-                prepare_last_lines()
-            if 0 <= step - TURN_LAG < PAIRS:
-                turn(2 * (step - TURN_LAG))
-                turn(2 * (step - TURN_LAG) + 1)
-
-        for i in range(TOKEN_TILES):
-            for h in range(FFN_HALVES):
+        def last_lines(h):
+            for i in range(TOKEN_TILES):
                 biased = work.tile([P, BANK], F32, tag="biased")
                 nc.vector.tensor_tensor(
                     out=biased[:], in0=acc[i][h][:], in1=bias_all[:, BANK * h : BANK * (h + 1)], op=ALU.add
@@ -232,3 +222,23 @@ def tile_transformerconvblock_pb_k_kernel(
                 result = work.tile([P, BANK], F32, tag="result")
                 nc.scalar.activation(out=result[:], in_=biased[:], func=ACT.Relu, scale=ffn_scale[:, 0:1])
                 nc.sync.dma_start(out=out_rows[P * i : P * (i + 1), BANK * h : BANK * (h + 1)], in_=result[:])
+
+        for step in range(STEPS):
+            for half in range(2):
+                if step < PAIRS:
+                    stage1(2 * step + half)
+                if 1 <= step <= PAIRS:
+                    quantise(2 * (step - 1) + half)
+                if 0 <= 2 * step - STAGE2_LAG + half < GROUPS - TAPERED:
+                    for h in range(FFN_HALVES):
+                        stage2(2 * step - STAGE2_LAG + half, h)
+            if step == 1:
+                prepare_last_lines()
+            if step < PAIRS:
+                turn(2 * step)
+                turn(2 * step + 1)
+
+        for h in range(FFN_HALVES):
+            for group in range(GROUPS - TAPERED, GROUPS):
+                stage2(group, h)
+            last_lines(h)

@@ -58,11 +58,20 @@ def tile_transformerconvblock_pb_k_kernel(
         identity = resident.tile([P, P], F32)
         make_identity(nc, identity[:])
 
+        for block in range(GROUPS // PLANES):
+            for quadrant in range(4):
+                nc.gpsimd.dma_start(
+                    out=ffn_planes[block][32 * quadrant : 32 * quadrant + 16, :].bitcast(F32),
+                    in_=ffn1_w_scales[
+                        PLANES * block : PLANES * (block + 1), 4 * quadrant : 4 * quadrant + 4, :
+                    ].bitcast(F32),
+                )
+
         attn_bf16 = resident.tile([P, 1], BF16)
         ffn_bf16 = resident.tile([P, 1], BF16)
         nc.scalar.dma_start(out=attn_bf16[:], in_=scale_attn.partition_broadcast(P))
-        nc.gpsimd.dma_start(out=bias_row[0:1, :], in_=ffn1_b.unsqueeze(0))
-        nc.gpsimd.dma_start(out=ffn_bf16[:], in_=scale_ffn.partition_broadcast(P))
+        nc.scalar.dma_start(out=ffn_bf16[:], in_=scale_ffn.partition_broadcast(P))
+        nc.scalar.dma_start(out=bias_row[0:1, :], in_=ffn1_b.unsqueeze(0))
 
         o_sb = resident.tile([P, TOKEN_TILES, K_PASS], BF16)
         nc.sync.dma_start(out=o_sb[:], in_=o_rows)
@@ -87,14 +96,6 @@ def tile_transformerconvblock_pb_k_kernel(
                 xn_sb.append(xn_pair)
             for group in (2 * step - STAGE2_LAG, 2 * step - STAGE2_LAG + 1):
                 if 0 <= group < GROUPS - TAPERED:
-                    if group % PLANES == 0:
-                        for quadrant in range(4):
-                            nc.sync.dma_start(
-                                out=ffn_planes[group // PLANES][32 * quadrant : 32 * quadrant + 16, :].bitcast(I32),
-                                in_=ffn1_w_scales[
-                                    group : group + PLANES, 4 * quadrant : 4 * quadrant + 4, :
-                                ].bitcast(I32),
-                            )
                     whole = resident.tile([P, 4 * FFN], U8, name="ffn%d" % group, align_bytes=64)
                     nc.sync.dma_start(out=whole[:].bitcast(I32), in_=ffn_words_in[:, group, :])
                     for h in range(FFN_HALVES):

@@ -46,18 +46,23 @@ def tile_transformerconvblock_pb_k_kernel(
     ) as psum_turned, tc.psum_pool(name="psum_acc", bufs=1) as psum_acc:
         wo_planes = resident.tile([P, CHANNELS // PLANES], U8, align_bytes=64)
         nc.vector.memset(wo_planes[:].bitcast(I32), 0)
+        bias_row = resident.tile([P, FFN], BF16)
+        nc.vector.memset(bias_row[:].bitcast(I32), 0)
         ffn_planes = []
         for block in range(GROUPS // PLANES):
             block_planes = resident.tile([P, FFN], U8, name="ffn_planes%d" % block, align_bytes=64)
             nc.vector.memset(block_planes[:].bitcast(I32), 0)
             ffn_planes.append(block_planes)
-        bias_row = resident.tile([P, FFN], BF16)
-        nc.vector.memset(bias_row[:], 0.0)
         ones = resident.tile([P, P], BF16)
         nc.vector.memset(ones[:], 1.0)
         identity = resident.tile([P, P], F32)
         make_identity(nc, identity[:])
 
+        attn_bf16 = resident.tile([P, 1], BF16)
+        ffn_bf16 = resident.tile([P, 1], BF16)
+        nc.scalar.dma_start(out=attn_bf16[:], in_=scale_attn.partition_broadcast(P))
+        nc.gpsimd.dma_start(out=ffn_bf16[:], in_=scale_ffn.partition_broadcast(P))
+        nc.gpsimd.dma_start(out=bias_row[0:1, :], in_=ffn1_b.unsqueeze(0))
         for block in range(GROUPS // PLANES):
             for quadrant in range(4):
                 nc.gpsimd.dma_start(
@@ -66,12 +71,6 @@ def tile_transformerconvblock_pb_k_kernel(
                         PLANES * block : PLANES * (block + 1), 4 * quadrant : 4 * quadrant + 4, :
                     ].bitcast(F32),
                 )
-
-        attn_bf16 = resident.tile([P, 1], BF16)
-        ffn_bf16 = resident.tile([P, 1], BF16)
-        nc.scalar.dma_start(out=attn_bf16[:], in_=scale_attn.partition_broadcast(P))
-        nc.scalar.dma_start(out=ffn_bf16[:], in_=scale_ffn.partition_broadcast(P))
-        nc.scalar.dma_start(out=bias_row[0:1, :], in_=ffn1_b.unsqueeze(0))
 
         o_sb = resident.tile([P, TOKEN_TILES, K_PASS], BF16)
         nc.sync.dma_start(out=o_sb[:], in_=o_rows)
@@ -91,9 +90,14 @@ def tile_transformerconvblock_pb_k_kernel(
                 wo_pair = resident.tile([P, 4 * 2 * K_PASS], U8, name="wo%d" % step, align_bytes=64)
                 nc.sync.dma_start(out=wo_pair[:].bitcast(I32), in_=wo_words_in[:, channels])
                 wo_words.append(wo_pair)
-                xn_pair = resident.tile([P, TOKEN_TILES, 2 * K_PASS], BF16, name="xn%d" % step)
-                nc.sync.dma_start(out=xn_pair[:], in_=xn_rows[:, :, channels])
-                xn_sb.append(xn_pair)
+                if step < 2 or step % 2 == 0:
+                    width = (2 if step < 2 else 4) * K_PASS
+                    xn_part = resident.tile([P, TOKEN_TILES, width], BF16, name="xn%d" % step)
+                    nc.sync.dma_start(
+                        out=xn_part[:], in_=xn_rows[:, :, 2 * K_PASS * step : 2 * K_PASS * step + width]
+                    )
+                    for first in range(0, width, K_PASS):
+                        xn_sb.append(xn_part[:, :, first : first + K_PASS])
             for group in (2 * step - STAGE2_LAG, 2 * step - STAGE2_LAG + 1):
                 if 0 <= group < GROUPS - TAPERED:
                     whole = resident.tile([P, 4 * FFN], U8, name="ffn%d" % group, align_bytes=64)
@@ -164,7 +168,7 @@ def tile_transformerconvblock_pb_k_kernel(
                     start=True,
                     stop=True,
                 )
-                residual = xn_sb[pair][:, i, K_PASS * half : K_PASS * (half + 1)]
+                residual = xn_sb[group][:, i, :]
                 for u in range(2):
                     nc.vector.scalar_tensor_tensor(
                         out=z[:, i, u, :].rearrange("k (p e) -> k p e", e=2),

@@ -63,7 +63,7 @@ def tile_transformerconvblock_pb_k_kernel(
         nc.scalar.dma_start(out=attn_bf16[:], in_=scale_attn.partition_broadcast(P))
         nc.gpsimd.dma_start(out=ffn_bf16[:], in_=scale_ffn.partition_broadcast(P))
         nc.gpsimd.dma_start(out=bias_row[0:1, :], in_=ffn1_b.unsqueeze(0))
-        for block in range(GROUPS // PLANES):
+        for block in range(1, GROUPS // PLANES):
             for quadrant in range(4):
                 nc.gpsimd.dma_start(
                     out=ffn_planes[block][32 * quadrant : 32 * quadrant + 16, :].bitcast(F32),
@@ -100,6 +100,12 @@ def tile_transformerconvblock_pb_k_kernel(
                         xn_sb.append(xn_part[:, :, first : first + K_PASS])
             for group in (2 * step - STAGE2_LAG, 2 * step - STAGE2_LAG + 1):
                 if 0 <= group < GROUPS - TAPERED:
+                    if group == 0:
+                        for quadrant in range(4):
+                            nc.sync.dma_start(
+                                out=ffn_planes[0][32 * quadrant : 32 * quadrant + 16, :].bitcast(I32),
+                                in_=ffn1_w_scales[0:PLANES, 4 * quadrant : 4 * quadrant + 4, :].bitcast(I32),
+                            )
                     whole = resident.tile([P, 4 * FFN], U8, name="ffn%d" % group, align_bytes=64)
                     nc.sync.dma_start(out=whole[:].bitcast(I32), in_=ffn_words_in[:, group, :])
                     for h in range(FFN_HALVES):

@@ -44,13 +44,13 @@ def tile_transformerconvblock_pb_k_kernel(
     ) as work, tc.psum_pool(name="psum_stage1", bufs=2) as psum_stage1, tc.psum_pool(
         name="psum_turned", bufs=2
     ) as psum_turned, tc.psum_pool(name="psum_acc", bufs=1) as psum_acc:
-        wo_planes = resident.tile([P, CHANNELS // PLANES], U8, align_bytes=64)
+        wo_planes = resident.tile([P, CHANNELS // PLANES], U8, align_bytes=256)
         nc.vector.memset(wo_planes[:].bitcast(I32), 0)
         bias_row = resident.tile([P, FFN], BF16)
         nc.vector.memset(bias_row[:].bitcast(I32), 0)
         ffn_planes = []
         for block in range(GROUPS // PLANES):
-            block_planes = resident.tile([P, FFN], U8, name="ffn_planes%d" % block, align_bytes=64)
+            block_planes = resident.tile([P, FFN], U8, name="ffn_planes%d" % block, align_bytes=256)
             nc.vector.memset(block_planes[:].bitcast(I32), 0)
             ffn_planes.append(block_planes)
         ones = resident.tile([P, P], BF16)
@@ -87,7 +87,7 @@ def tile_transformerconvblock_pb_k_kernel(
         for step in range(STEPS):
             if step < PAIRS:
                 channels = slice(2 * K_PASS * step, 2 * K_PASS * (step + 1))
-                wo_pair = resident.tile([P, 4 * 2 * K_PASS], U8, name="wo%d" % step, align_bytes=64)
+                wo_pair = resident.tile([P, 4 * 2 * K_PASS], U8, name="wo%d" % step, align_bytes=256)
                 nc.sync.dma_start(out=wo_pair[:].bitcast(I32), in_=wo_words_in[:, channels])
                 wo_words.append(wo_pair)
                 if step < 2 or step % 2 == 0:
@@ -106,13 +106,13 @@ def tile_transformerconvblock_pb_k_kernel(
                                 out=ffn_planes[0][32 * quadrant : 32 * quadrant + 16, :].bitcast(I32),
                                 in_=ffn1_w_scales[0:PLANES, 4 * quadrant : 4 * quadrant + 4, :].bitcast(I32),
                             )
-                    whole = resident.tile([P, 4 * FFN], U8, name="ffn%d" % group, align_bytes=64)
+                    whole = resident.tile([P, 4 * FFN], U8, name="ffn%d" % group, align_bytes=256)
                     nc.sync.dma_start(out=whole[:].bitcast(I32), in_=ffn_words_in[:, group, :])
                     for h in range(FFN_HALVES):
                         ffn_words[(group, h)] = whole[:, 4 * BANK * h : 4 * BANK * (h + 1)]
         for h in range(FFN_HALVES):
             for group in range(GROUPS - TAPERED, GROUPS):
-                part = resident.tile([P, 4 * BANK], U8, name="ffn%d_%d" % (group, h), align_bytes=64)
+                part = resident.tile([P, 4 * BANK], U8, name="ffn%d_%d" % (group, h), align_bytes=256)
                 nc.sync.dma_start(out=part[:].bitcast(I32), in_=ffn_words_in[:, group, BANK * h : BANK * (h + 1)])
                 ffn_words[(group, h)] = part[:]
 
@@ -126,13 +126,13 @@ def tile_transformerconvblock_pb_k_kernel(
                 nc.tensor.transpose(
                     o_turned[:, u, P * i : P * (i + 1)], o_as_words[:, u : K_PASS // 2 : 2], identity[:]
                 )
-        o_grouped = work.tile([P, TOKENS, 2, 2], BF16, tag="grouped", align_bytes=64)
+        o_grouped = work.tile([P, TOKENS, 2, 2], BF16, tag="grouped", align_bytes=256)
         nc.vector.tensor_copy(
             out=o_grouped[:].rearrange("p k u e -> p k (u e)").bitcast(F32),
             in_=o_turned[:].rearrange("p u k -> p k u"),
         )
-        o_codes = resident.tile([P, TOKENS], U32, align_bytes=64)
-        o_plane = resident.tile([P, TOKENS], U8, align_bytes=64)
+        o_codes = resident.tile([P, TOKENS], U32, align_bytes=256)
+        o_plane = resident.tile([P, TOKENS], U8, align_bytes=256)
         nc.vector.quantize_mx(
             out=o_codes[:].bitcast(FP8X4),
             scales=o_plane[:],
@@ -192,7 +192,7 @@ def tile_transformerconvblock_pb_k_kernel(
             for i in range(TOKEN_TILES):
                 for u in range(2):
                     nc.tensor.transpose(turned[:, u, P * i : P * (i + 1)], z[:, i, u, :].bitcast(F32), identity[:])
-            y = work.tile([P, TOKENS, 2, 2], BF16, tag="grouped", align_bytes=64)
+            y = work.tile([P, TOKENS, 2, 2], BF16, tag="grouped", align_bytes=256)
             nc.scalar.activation(
                 out=y[:],
                 in_=turned[:].bitcast(BF16).rearrange("p u (k e) -> p k u e", e=2),
@@ -201,8 +201,8 @@ def tile_transformerconvblock_pb_k_kernel(
             grouped[group] = y
 
         def quantise(group):
-            codes = resident.tile([P, TOKENS], U32, name="y_codes%d" % group, align_bytes=64)
-            plane = resident.tile([P, TOKENS], U8, name="y_plane%d" % group, align_bytes=64)
+            codes = resident.tile([P, TOKENS], U32, name="y_codes%d" % group, align_bytes=256)
+            plane = resident.tile([P, TOKENS], U8, name="y_plane%d" % group, align_bytes=256)
             nc.vector.quantize_mx(
                 out=codes[:].bitcast(FP8X4),
                 scales=plane[:],

@@ -44,10 +44,14 @@ def tile_transformerconvblock_pb_k_kernel(
     ) as work, tc.psum_pool(name="psum_stage1", bufs=2) as psum_stage1, tc.psum_pool(
         name="psum_turned", bufs=2
     ) as psum_turned, tc.psum_pool(name="psum_acc", bufs=1) as psum_acc:
+        attn_row = resident.tile([P, 2], BF16)
+        nc.vector.memset(attn_row[:], 0.0)
         wo_planes = resident.tile([P, CHANNELS // PLANES], U8, align_bytes=256)
         nc.vector.memset(wo_planes[:].bitcast(I32), 0)
         bias_row = resident.tile([P, FFN], BF16)
         nc.vector.memset(bias_row[:].bitcast(I32), 0)
+        ffn_row = resident.tile([P, 2], BF16)
+        nc.vector.memset(ffn_row[:], 0.0)
         ffn_planes = []
         for block in range(GROUPS // PLANES):
             block_planes = resident.tile([P, FFN], U8, name="ffn_planes%d" % block, align_bytes=256)
@@ -58,10 +62,8 @@ def tile_transformerconvblock_pb_k_kernel(
         identity = resident.tile([P, P], F32)
         make_identity(nc, identity[:])
 
-        attn_bf16 = resident.tile([P, 1], BF16)
-        ffn_bf16 = resident.tile([P, 1], BF16)
-        nc.scalar.dma_start(out=attn_bf16[:], in_=scale_attn.partition_broadcast(P))
-        nc.gpsimd.dma_start(out=ffn_bf16[:], in_=scale_ffn.partition_broadcast(P))
+        nc.scalar.dma_start(out=attn_row[0:1, 0:1], in_=scale_attn.unsqueeze(0))
+        nc.gpsimd.dma_start(out=ffn_row[0:1, 0:1], in_=scale_ffn.unsqueeze(0))
         nc.gpsimd.dma_start(out=bias_row[0:1, :], in_=ffn1_b.unsqueeze(0))
         for block in range(1, GROUPS // PLANES):
             for quadrant in range(4):
@@ -116,9 +118,6 @@ def tile_transformerconvblock_pb_k_kernel(
                 nc.sync.dma_start(out=part[:].bitcast(I32), in_=ffn_words_in[:, group, BANK * h : BANK * (h + 1)])
                 ffn_words[(group, h)] = part[:]
 
-        attn_scale = resident.tile([P, 1], F32)
-        nc.vector.tensor_copy(out=attn_scale[:], in_=attn_bf16[:])
-
         o_turned = psum_turned.tile([P, 2, TOKENS], F32, tag="turned")
         for i in range(TOKEN_TILES):
             o_as_words = o_sb[:, i, :].bitcast(F32)
@@ -126,6 +125,8 @@ def tile_transformerconvblock_pb_k_kernel(
                 nc.tensor.transpose(
                     o_turned[:, u, P * i : P * (i + 1)], o_as_words[:, u : K_PASS // 2 : 2], identity[:]
                 )
+        attn_product = psum_stage1.tile([P, 2], F32, tag="stage1")
+        nc.tensor.matmul(out=attn_product[:], lhsT=ones[:], rhs=attn_row[:], start=True, stop=True)
         o_grouped = work.tile([P, TOKENS, 2, 2], BF16, tag="grouped", align_bytes=256)
         nc.vector.tensor_copy(
             out=o_grouped[:].rearrange("p k u e -> p k (u e)").bitcast(F32),
@@ -138,6 +139,9 @@ def tile_transformerconvblock_pb_k_kernel(
             scales=o_plane[:],
             in_=o_grouped[:].rearrange("p k u e -> p (k u e)"),
         )
+
+        attn_scale = resident.tile([P, 1], F32)
+        nc.vector.tensor_copy(out=attn_scale[:], in_=attn_product[:, 0:1])
 
         summed = {}
         grouped = {}
@@ -152,7 +156,8 @@ def tile_transformerconvblock_pb_k_kernel(
         ffn_scale = resident.tile([P, 1], F32)
 
         def prepare_last_lines():
-            nc.vector.tensor_copy(out=ffn_scale[:], in_=ffn_bf16[:])
+            nc.tensor.matmul(out=acc[1][0][:, 0:2], lhsT=ones[:], rhs=ffn_row[:], start=True, stop=True)
+            nc.scalar.copy(out=ffn_scale[:], in_=acc[1][0][:, 0:1])
             for h in range(FFN_HALVES):
                 nc.tensor.matmul(
                     out=acc[0][h][:], lhsT=ones[:], rhs=bias_row[:, BANK * h : BANK * (h + 1)], start=True, stop=True

@@ -21,9 +21,10 @@ FFN = 1024
 BANK = 512
 FFN_HALVES = FFN // BANK
 PLANES = 4
-STAGE2_LAG = 5
+TURN_LAG = 2
+STAGE2_LAG = 6
 TAPERED = 2
-STEPS = (GROUPS - TAPERED + STAGE2_LAG + 1) // 2
+STEPS = (GROUPS - TAPERED + STAGE2_LAG - TURN_LAG) // 2
 
 FLOPS = 2 * TOKENS * K_PASS * CHANNELS + 2 * TOKENS * CHANNELS * FFN
 
@@ -86,32 +87,34 @@ def tile_transformerconvblock_pb_k_kernel(
         wo_words = []
         ffn_words = {}
 
-        for step in range(STEPS):
-            if step < PAIRS:
-                channels = slice(2 * K_PASS * step, 2 * K_PASS * (step + 1))
-                wo_pair = resident.tile([P, 4 * 2 * K_PASS], U8, name="wo%d" % step, align_bytes=256)
+        def load_ffn(group):
+            if group == 0:
+                for quadrant in range(4):
+                    nc.sync.dma_start(
+                        out=ffn_planes[0][32 * quadrant : 32 * quadrant + 16, :].bitcast(I32),
+                        in_=ffn1_w_scales[0:PLANES, 4 * quadrant : 4 * quadrant + 4, :].bitcast(I32),
+                    )
+            whole = resident.tile([P, 4 * FFN], U8, name="ffn%d" % group, align_bytes=256)
+            nc.sync.dma_start(out=whole[:].bitcast(I32), in_=ffn_words_in[:, group, :])
+            for h in range(FFN_HALVES):
+                ffn_words[(group, h)] = whole[:, 4 * BANK * h : 4 * BANK * (h + 1)]
+
+        for pair in range((GROUPS - TAPERED + STAGE2_LAG) // 2):
+            channels = slice(2 * K_PASS * pair, 2 * K_PASS * (pair + 1))
+            group = 2 * pair - STAGE2_LAG
+            if pair < PAIRS:
+                wo_pair = resident.tile([P, 4 * 2 * K_PASS], U8, name="wo%d" % pair, align_bytes=256)
                 nc.sync.dma_start(out=wo_pair[:].bitcast(I32), in_=wo_words_in[:, channels])
                 wo_words.append(wo_pair)
-                if step < 2 or step % 2 == 0:
-                    width = (2 if step < 2 else 4) * K_PASS
-                    xn_part = resident.tile([P, TOKEN_TILES, width], BF16, name="xn%d" % step)
-                    nc.sync.dma_start(
-                        out=xn_part[:], in_=xn_rows[:, :, 2 * K_PASS * step : 2 * K_PASS * step + width]
-                    )
-                    for first in range(0, width, K_PASS):
-                        xn_sb.append(xn_part[:, :, first : first + K_PASS])
-            for group in (2 * step - STAGE2_LAG, 2 * step - STAGE2_LAG + 1):
-                if 0 <= group < GROUPS - TAPERED:
-                    if group == 0:
-                        for quadrant in range(4):
-                            nc.sync.dma_start(
-                                out=ffn_planes[0][32 * quadrant : 32 * quadrant + 16, :].bitcast(I32),
-                                in_=ffn1_w_scales[0:PLANES, 4 * quadrant : 4 * quadrant + 4, :].bitcast(I32),
-                            )
-                    whole = resident.tile([P, 4 * FFN], U8, name="ffn%d" % group, align_bytes=256)
-                    nc.sync.dma_start(out=whole[:].bitcast(I32), in_=ffn_words_in[:, group, :])
-                    for h in range(FFN_HALVES):
-                        ffn_words[(group, h)] = whole[:, 4 * BANK * h : 4 * BANK * (h + 1)]
+            if group >= 0:
+                load_ffn(group)
+            if pair < PAIRS:
+                xn_pair = resident.tile([P, TOKEN_TILES, 2 * K_PASS], BF16, name="xn%d" % pair)
+                nc.sync.dma_start(out=xn_pair[:], in_=xn_rows[:, :, channels])
+                for first in range(0, 2 * K_PASS, K_PASS):
+                    xn_sb.append(xn_pair[:, :, first : first + K_PASS])
+            if group >= 0:
+                load_ffn(group + 1)
         for h in range(FFN_HALVES):
             for group in range(GROUPS - TAPERED, GROUPS):
                 part = resident.tile([P, 4 * BANK], U8, name="ffn%d_%d" % (group, h), align_bytes=256)
@@ -169,7 +172,8 @@ def tile_transformerconvblock_pb_k_kernel(
             plane, quarter = divmod(group, PLANES)
             z = work.tile([P, TOKEN_TILES, 2, 2 * P], BF16, tag="summed")
             for i in range(TOKEN_TILES):
-                product = psum_stage1.tile([P, BANK], F32, tag="stage1")
+                borrow = group in (1, 2)
+                product = acc[i][group - 1] if borrow else psum_stage1.tile([P, BANK], F32, tag="stage1")
                 nc.tensor.matmul_mx(
                     out=product[:],
                     lhsT=o_codes[:, P * i : P * (i + 1)].bitcast(FP8X4),
@@ -230,29 +234,34 @@ def tile_transformerconvblock_pb_k_kernel(
                 )
 
         def last_lines(h):
+            width = BANK if h == 0 else BANK // 2
             for i in range(TOKEN_TILES):
-                biased = work.tile([P, BANK], F32, tag="biased")
-                nc.vector.tensor_tensor(
-                    out=biased[:], in0=acc[i][h][:], in1=bias_all[:, BANK * h : BANK * (h + 1)], op=ALU.add
-                )
-                result = work.tile([P, BANK], F32, tag="result")
-                nc.scalar.activation(out=result[:], in_=biased[:], func=ACT.Relu, scale=ffn_scale[:, 0:1])
-                nc.sync.dma_start(out=out_rows[P * i : P * (i + 1), BANK * h : BANK * (h + 1)], in_=result[:])
+                for first in range(0, BANK, width):
+                    columns = slice(BANK * h + first, BANK * h + first + width)
+                    biased = work.tile([P, width], F32, tag="biased%d" % h)
+                    nc.vector.tensor_tensor(
+                        out=biased[:], in0=acc[i][h][:, first : first + width], in1=bias_all[:, columns], op=ALU.add
+                    )
+                    result = work.tile([P, width], F32, tag="result%d" % h)
+                    nc.scalar.activation(out=result[:], in_=biased[:], func=ACT.Relu, scale=ffn_scale[:, 0:1])
+                    nc.sync.dma_start(out=out_rows[P * i : P * (i + 1), columns], in_=result[:])
 
+        for group in range(TURN_LAG):
+            stage1(group)
         for step in range(STEPS):
             for half in range(2):
-                if step < PAIRS:
-                    stage1(2 * step + half)
-                if 1 <= step <= PAIRS:
-                    quantise(2 * (step - 1) + half)
-                if 0 <= 2 * step - STAGE2_LAG + half < GROUPS - TAPERED:
+                if 2 * step + TURN_LAG + half < GROUPS:
+                    stage1(2 * step + TURN_LAG + half)
+                if 0 <= 2 * step - 1 + half < GROUPS:
+                    quantise(2 * step - 1 + half)
+                if 0 <= 2 * step + TURN_LAG - STAGE2_LAG + half < GROUPS - TAPERED:
                     for h in range(FFN_HALVES):
-                        stage2(2 * step - STAGE2_LAG + half, h)
+                        stage2(2 * step + TURN_LAG - STAGE2_LAG + half, h)
+                if half == 0 and step < PAIRS:
+                    turn(2 * step)
+                    turn(2 * step + 1)
             if step == 1:
                 prepare_last_lines()
-            if step < PAIRS:
-                turn(2 * step)
-                turn(2 * step + 1)
 
         for h in range(FFN_HALVES):
             for group in range(GROUPS - TAPERED, GROUPS):

@@ -220,18 +220,19 @@ def tile_transformerconvblock_pb_k_kernel(
             y_codes[group] = codes
             y_planes[group] = plane
 
-        def stage2(group, h):
+        def stage2(group, halves):
             block, plane = divmod(group, PLANES)
             for i in range(TOKEN_TILES):
-                nc.tensor.matmul_mx(
-                    out=acc[i][h][:],
-                    lhsT=y_codes[group][:, P * i : P * (i + 1)].bitcast(FP8X4),
-                    lhsT_scale=y_planes[group][:, P * i : P * (i + 1)],
-                    rhs=ffn_words[(group, h)].bitcast(FP8X4),
-                    rhs_scale=ffn_planes[block][4 * plane : P, BANK * h : BANK * (h + 1)],
-                    start=(group == 0),
-                    stop=(group == GROUPS - 1),
-                )
+                for h in halves:
+                    nc.tensor.matmul_mx(
+                        out=acc[i][h][:],
+                        lhsT=y_codes[group][:, P * i : P * (i + 1)].bitcast(FP8X4),
+                        lhsT_scale=y_planes[group][:, P * i : P * (i + 1)],
+                        rhs=ffn_words[(group, h)].bitcast(FP8X4),
+                        rhs_scale=ffn_planes[block][4 * plane : P, BANK * h : BANK * (h + 1)],
+                        start=(group == 0),
+                        stop=(group == GROUPS - 1),
+                    )
 
         def last_lines(h):
             width = BANK if h == 0 else BANK // 2
@@ -255,8 +256,7 @@ def tile_transformerconvblock_pb_k_kernel(
                 if 0 <= 2 * step - 1 + half < GROUPS:
                     quantise(2 * step - 1 + half)
                 if 0 <= 2 * step + TURN_LAG - STAGE2_LAG + half < GROUPS - TAPERED:
-                    for h in range(FFN_HALVES):
-                        stage2(2 * step + TURN_LAG - STAGE2_LAG + half, h)
+                    stage2(2 * step + TURN_LAG - STAGE2_LAG + half, range(FFN_HALVES))
                 if half == 0 and step < PAIRS:
                     turn(2 * step)
                     turn(2 * step + 1)
@@ -265,5 +265,5 @@ def tile_transformerconvblock_pb_k_kernel(
 
         for h in range(FFN_HALVES):
             for group in range(GROUPS - TAPERED, GROUPS):
-                stage2(group, h)
+                stage2(group, [h])
             last_lines(h)

import concourse.mybir as mybir
from concourse.masks import make_identity

F32 = mybir.dt.float32
BF16 = mybir.dt.bfloat16
I32 = mybir.dt.int32
U32 = mybir.dt.uint32
U8 = mybir.dt.uint8
FP8X4 = mybir.dt.float8_e4m3fn_x4
ALU = mybir.AluOpType
ACT = mybir.ActivationFunctionType

P = 128
TOKENS = 256
TOKEN_TILES = TOKENS // P
K_PASS = 4 * P
CHANNELS = 8192
GROUPS = CHANNELS // K_PASS
PAIRS = GROUPS // 2
FFN = 1024
BANK = 512
FFN_HALVES = FFN // BANK
PLANES = 4
TURN_LAG = 2
STAGE2_LAG = 6
TAPERED = 2
STEPS = (GROUPS - TAPERED + STAGE2_LAG - TURN_LAG) // 2

FLOPS = 2 * TOKENS * K_PASS * CHANNELS + 2 * TOKENS * CHANNELS * FFN


def tile_transformerconvblock_pb_k_kernel(
    tc, o, xn, W_O_words, W_O_scales, scale_attn, ffn1_w_words, ffn1_w_scales, ffn1_b, scale_ffn, out
):
    nc = tc.nc
    o_rows = o.flatten_outer_dims().rearrange("(i p) k -> p i k", p=P)
    xn_rows = xn.flatten_outer_dims().rearrange("(i p) c -> p i c", p=P)
    out_rows = out.flatten_outer_dims()
    wo_words_in = W_O_words.rearrange("g p n t -> (g p) (n t)").bitcast(I32)
    wo_scales_in = W_O_scales.rearrange("g q (k x) -> (g k) q x", k=PLANES)
    ffn_words_in = ffn1_w_words.rearrange("g p n t -> p g (n t)").bitcast(I32)

    with tc.manual_schedule(), tc.tile_pool(name="resident", bufs=1) as resident, tc.tile_pool(
        name="work", bufs=4
    ) as work, tc.psum_pool(name="psum_stage1", bufs=2) as psum_stage1, tc.psum_pool(
        name="psum_turned", bufs=2
    ) as psum_turned, tc.psum_pool(name="psum_acc", bufs=1) as psum_acc:
        attn_row = resident.tile([P, 2], BF16)
        nc.vector.memset(attn_row[:], 0.0)
        wo_planes = resident.tile([P, CHANNELS // PLANES], U8, align_bytes=256)
        nc.vector.memset(wo_planes[:].bitcast(I32), 0)
        bias_row = resident.tile([P, FFN], BF16)
        nc.vector.memset(bias_row[:].bitcast(I32), 0)
        ffn_row = resident.tile([P, 2], BF16)
        nc.vector.memset(ffn_row[:], 0.0)
        ffn_planes = []
        for block in range(GROUPS // PLANES):
            block_planes = resident.tile([P, FFN], U8, name="ffn_planes%d" % block, align_bytes=256)
            nc.vector.memset(block_planes[:].bitcast(I32), 0)
            ffn_planes.append(block_planes)
        ones = resident.tile([P, P], BF16)
        nc.vector.memset(ones[:], 1.0)
        identity = resident.tile([P, P], F32)
        make_identity(nc, identity[:])

        nc.scalar.dma_start(out=attn_row[0:1, 0:1], in_=scale_attn.unsqueeze(0))
        nc.gpsimd.dma_start(out=ffn_row[0:1, 0:1], in_=scale_ffn.unsqueeze(0))
        nc.gpsimd.dma_start(out=bias_row[0:1, :], in_=ffn1_b.unsqueeze(0))
        for block in range(1, GROUPS // PLANES):
            for quadrant in range(4):
                nc.gpsimd.dma_start(
                    out=ffn_planes[block][32 * quadrant : 32 * quadrant + 16, :].bitcast(F32),
                    in_=ffn1_w_scales[
                        PLANES * block : PLANES * (block + 1), 4 * quadrant : 4 * quadrant + 4, :
                    ].bitcast(F32),
                )

        o_sb = resident.tile([P, TOKEN_TILES, K_PASS], BF16)
        nc.sync.dma_start(out=o_sb[:], in_=o_rows)
        for quadrant in range(4):
            nc.sync.dma_start(
                out=wo_planes[32 * quadrant : 32 * quadrant + 16, :].bitcast(I32),
                in_=wo_scales_in[:, 4 * quadrant : 4 * quadrant + 4, :].bitcast(I32),
            )

        xn_sb = []
        wo_words = []
        ffn_words = {}

        def load_ffn(group):
            if group == 0:
                for quadrant in range(4):
                    nc.sync.dma_start(
                        out=ffn_planes[0][32 * quadrant : 32 * quadrant + 16, :].bitcast(I32),
                        in_=ffn1_w_scales[0:PLANES, 4 * quadrant : 4 * quadrant + 4, :].bitcast(I32),
                    )
            whole = resident.tile([P, 4 * FFN], U8, name="ffn%d" % group, align_bytes=256)
            nc.sync.dma_start(out=whole[:].bitcast(I32), in_=ffn_words_in[:, group, :])
            for h in range(FFN_HALVES):
                ffn_words[(group, h)] = whole[:, 4 * BANK * h : 4 * BANK * (h + 1)]

        for pair in range((GROUPS - TAPERED + STAGE2_LAG) // 2):
            channels = slice(2 * K_PASS * pair, 2 * K_PASS * (pair + 1))
            group = 2 * pair - STAGE2_LAG
            if pair < PAIRS:
                wo_pair = resident.tile([P, 4 * 2 * K_PASS], U8, name="wo%d" % pair, align_bytes=256)
                nc.sync.dma_start(out=wo_pair[:].bitcast(I32), in_=wo_words_in[:, channels])
                wo_words.append(wo_pair)
            if group >= 0:
                load_ffn(group)
            if pair < PAIRS:
                xn_pair = resident.tile([P, TOKEN_TILES, 2 * K_PASS], BF16, name="xn%d" % pair)
                nc.sync.dma_start(out=xn_pair[:], in_=xn_rows[:, :, channels])
                for first in range(0, 2 * K_PASS, K_PASS):
                    xn_sb.append(xn_pair[:, :, first : first + K_PASS])
            if group >= 0:
                load_ffn(group + 1)
        for h in range(FFN_HALVES):
            for group in range(GROUPS - TAPERED, GROUPS):
                part = resident.tile([P, 4 * BANK], U8, name="ffn%d_%d" % (group, h), align_bytes=256)
                nc.sync.dma_start(out=part[:].bitcast(I32), in_=ffn_words_in[:, group, BANK * h : BANK * (h + 1)])
                ffn_words[(group, h)] = part[:]

        o_turned = psum_turned.tile([P, 2, TOKENS], F32, tag="turned")
        for i in range(TOKEN_TILES):
            o_as_words = o_sb[:, i, :].bitcast(F32)
            for u in range(2):
                nc.tensor.transpose(
                    o_turned[:, u, P * i : P * (i + 1)], o_as_words[:, u : K_PASS // 2 : 2], identity[:]
                )
        attn_product = psum_stage1.tile([P, 2], F32, tag="stage1")
        nc.tensor.matmul(out=attn_product[:], lhsT=ones[:], rhs=attn_row[:], start=True, stop=True)
        o_grouped = work.tile([P, TOKENS, 2, 2], BF16, tag="grouped", align_bytes=256)
        nc.vector.tensor_copy(
            out=o_grouped[:].rearrange("p k u e -> p k (u e)").bitcast(F32),
            in_=o_turned[:].rearrange("p u k -> p k u"),
        )
        o_codes = resident.tile([P, TOKENS], U32, align_bytes=256)
        o_plane = resident.tile([P, TOKENS], U8, align_bytes=256)
        nc.vector.quantize_mx(
            out=o_codes[:].bitcast(FP8X4),
            scales=o_plane[:],
            in_=o_grouped[:].rearrange("p k u e -> p (k u e)"),
        )

        attn_scale = resident.tile([P, 1], F32)
        nc.vector.tensor_copy(out=attn_scale[:], in_=attn_product[:, 0:1])

        summed = {}
        grouped = {}
        y_codes = {}
        y_planes = {}
        acc = [
            [psum_acc.tile([P, BANK], F32, name="acc%d%d" % (i, h)) for h in range(FFN_HALVES)]
            for i in range(TOKEN_TILES)
        ]

        bias_all = resident.tile([P, FFN], F32)
        ffn_scale = resident.tile([P, 1], F32)

        def prepare_last_lines():
            nc.tensor.matmul(out=acc[1][0][:, 0:2], lhsT=ones[:], rhs=ffn_row[:], start=True, stop=True)
            nc.scalar.copy(out=ffn_scale[:], in_=acc[1][0][:, 0:1])
            for h in range(FFN_HALVES):
                nc.tensor.matmul(
                    out=acc[0][h][:], lhsT=ones[:], rhs=bias_row[:, BANK * h : BANK * (h + 1)], start=True, stop=True
                )
                nc.scalar.copy(out=bias_all[:, BANK * h : BANK * (h + 1)], in_=acc[0][h][:])

        def stage1(group):
            pair, half = divmod(group, 2)
            plane, quarter = divmod(group, PLANES)
            z = work.tile([P, TOKEN_TILES, 2, 2 * P], BF16, tag="summed")
            for i in range(TOKEN_TILES):
                borrow = group in (1, 2)
                product = acc[i][group - 1] if borrow else psum_stage1.tile([P, BANK], F32, tag="stage1")
                nc.tensor.matmul_mx(
                    out=product[:],
                    lhsT=o_codes[:, P * i : P * (i + 1)].bitcast(FP8X4),
                    lhsT_scale=o_plane[:, P * i : P * (i + 1)],
                    rhs=wo_words[pair][:, 4 * K_PASS * half : 4 * K_PASS * (half + 1)].bitcast(FP8X4),
                    rhs_scale=wo_planes[4 * plane : P, K_PASS * quarter : K_PASS * (quarter + 1)],
                    start=True,
                    stop=True,
                )
                residual = xn_sb[group][:, i, :]
                for u in range(2):
                    nc.vector.scalar_tensor_tensor(
                        out=z[:, i, u, :].rearrange("k (p e) -> k p e", e=2),
                        in0=product[:].rearrange("k (p u e) -> k u p e", u=2, e=2)[:, u],
                        scalar=attn_scale[:, 0:1],
                        in1=residual.rearrange("k (p u e) -> k u p e", u=2, e=2)[:, u],
                        op0=ALU.mult,
                        op1=ALU.add,
                    )
            summed[group] = z

        def turn(group):
            z = summed[group]
            turned = psum_turned.tile([P, 2, TOKENS], F32, tag="turned")
            for i in range(TOKEN_TILES):
                for u in range(2):
                    nc.tensor.transpose(turned[:, u, P * i : P * (i + 1)], z[:, i, u, :].bitcast(F32), identity[:])
            y = work.tile([P, TOKENS, 2, 2], BF16, tag="grouped", align_bytes=256)
            nc.scalar.activation(
                out=y[:],
                in_=turned[:].bitcast(BF16).rearrange("p u (k e) -> p k u e", e=2),
                func=ACT.Relu,
            )
            grouped[group] = y

        def quantise(group):
            codes = resident.tile([P, TOKENS], U32, name="y_codes%d" % group, align_bytes=256)
            plane = resident.tile([P, TOKENS], U8, name="y_plane%d" % group, align_bytes=256)
            nc.vector.quantize_mx(
                out=codes[:].bitcast(FP8X4),
                scales=plane[:],
                in_=grouped[group][:].rearrange("p k u e -> p (k u e)"),
            )
            y_codes[group] = codes
            y_planes[group] = plane

        def stage2(group, halves):
            block, plane = divmod(group, PLANES)
            for i in range(TOKEN_TILES):
                for h in halves:
                    nc.tensor.matmul_mx(
                        out=acc[i][h][:],
                        lhsT=y_codes[group][:, P * i : P * (i + 1)].bitcast(FP8X4),
                        lhsT_scale=y_planes[group][:, P * i : P * (i + 1)],
                        rhs=ffn_words[(group, h)].bitcast(FP8X4),
                        rhs_scale=ffn_planes[block][4 * plane : P, BANK * h : BANK * (h + 1)],
                        start=(group == 0),
                        stop=(group == GROUPS - 1),
                    )

        def last_lines(h):
            width = BANK if h == 0 else BANK // 2
            for i in range(TOKEN_TILES):
                for first in range(0, BANK, width):
                    columns = slice(BANK * h + first, BANK * h + first + width)
                    biased = work.tile([P, width], F32, tag="biased%d" % h)
                    nc.vector.tensor_tensor(
                        out=biased[:], in0=acc[i][h][:, first : first + width], in1=bias_all[:, columns], op=ALU.add
                    )
                    result = work.tile([P, width], F32, tag="result%d" % h)
                    nc.scalar.activation(out=result[:], in_=biased[:], func=ACT.Relu, scale=ffn_scale[:, 0:1])
                    nc.sync.dma_start(out=out_rows[P * i : P * (i + 1), columns], in_=result[:])

        for group in range(TURN_LAG):
            stage1(group)
        for step in range(STEPS):
            for half in range(2):
                if 2 * step + TURN_LAG + half < GROUPS:
                    stage1(2 * step + TURN_LAG + half)
                if 0 <= 2 * step - 1 + half < GROUPS:
                    quantise(2 * step - 1 + half)
                if 0 <= 2 * step + TURN_LAG - STAGE2_LAG + half < GROUPS - TAPERED:
                    stage2(2 * step + TURN_LAG - STAGE2_LAG + half, range(FFN_HALVES))
                if half == 0 and step < PAIRS:
                    turn(2 * step)
                    turn(2 * step + 1)
            if step == 1:
                prepare_last_lines()

        for h in range(FFN_HALVES):
            for group in range(GROUPS - TAPERED, GROUPS):
                stage2(group, [h])
            last_lines(h)
